import numpy as np
import ml_dtypes


def mxq(x, axis, fmt="e4m3"):
    dtype, down = {"e4m3": (ml_dtypes.float8_e4m3fn, 7), "e5m2": (ml_dtypes.float8_e5m2, 14)}[fmt]
    v = np.moveaxis(np.asarray(x, np.float32).astype(ml_dtypes.bfloat16).astype(np.float64), axis, -1)
    blocks = v.reshape(v.shape[:-1] + (-1, 32))
    amax = np.abs(blocks).max(-1, keepdims=True)
    byte = np.maximum(np.where(amax > 0, np.frexp(amax)[1] - 1 + 127, 0) - down, 1)
    scale = np.exp2(byte - 127.0)
    codes = (blocks / scale).astype(np.float32).astype(dtype).astype(np.float64)
    return np.moveaxis((codes * scale).reshape(v.shape), -1, axis)


WIDE = False


def mx_kscale(k):
    if not WIDE:
        return np.ones(k)
    levels = np.array([10, -10, 5, -5, 0])
    a = np.random.permutation(np.resize(levels, k // 512 * 4)).reshape(k // 512, 4)
    idx = np.arange(k)
    return np.exp2(a[idx // 512, idx % 128 // 32])


BF16 = ml_dtypes.bfloat16


def bf(x):
    return np.asarray(x, np.float32).astype(BF16)


def f64(x):
    return np.asarray(x).astype(np.float64)


E2M1 = np.array([0.0, 0.5, 1.0, 1.5, 2.0, 3.0, 4.0, 6.0, -0.0, -0.5, -1.0, -1.5, -2.0, -3.0, -4.0, -6.0])


def pack_weight(w, fmt):
    k, n = w.shape
    w = f64(bf(w)).reshape(k // 32, 32, n)
    amax = np.abs(w).max(1)
    if fmt == "e4m3":
        byte = np.frexp(amax)[1] - 1 + 127 - 7
    else:
        mant, ex = np.frexp(amax / 6.0)
        byte = np.where(mant > 0.5, ex, ex - 1) + 127
    byte = np.clip(np.where(amax > 0, byte, 1), 1, 254)
    scaled = (w * np.exp2(127.0 - byte)[:, None, :]).reshape(k, n).astype(np.float32)
    by_word = np.ascontiguousarray(scaled.reshape(k // 512, 128, 4, n).transpose(0, 1, 3, 2))
    if fmt == "e4m3":
        words = by_word.astype(ml_dtypes.float8_e4m3fn).view(np.uint8)
    else:
        c = by_word.astype(ml_dtypes.float4_e2m1fn).view(np.uint8) & 0xF
        words = c[..., 0::2] | (c[..., 1::2] << 4)
    return np.ascontiguousarray(words), np.ascontiguousarray(byte.astype(np.uint8).reshape(k // 512, 16, n))


def unpack_weight(words, scales, fmt):
    g, p, n, _ = words.shape
    if fmt == "e4m3":
        vals = np.ascontiguousarray(words).view(ml_dtypes.float8_e4m3fn).astype(np.float64)
    else:
        nib = np.empty((g, p, n, 4), np.uint8)
        nib[..., 0::2] = words & 0xF
        nib[..., 1::2] = words >> 4
        vals = E2M1[nib]
    vals = vals * np.repeat(np.exp2(scales.astype(np.float64) - 127.0), 8, axis=1)[..., None]
    return vals.transpose(0, 1, 3, 2).reshape(g * 512, n)


B, S, K, N = 2, 64, 16384, 1024
FMT = "e4m3"


def setup_inputs():
    s = mx_kscale(K)
    input = bf(np.random.standard_normal((B, S, K)) * s)
    weight = np.random.standard_normal((N, K)) / np.sqrt(K) / s[None, :]
    words, scales = pack_weight(np.ascontiguousarray(weight.T), FMT)
    bias = bf(np.random.standard_normal(N) * 0.5)
    return {"input": input,
            "weight_words": words,
            "weight_scales": scales,
            "bias": bias}


def reference(input, weight_words, weight_scales, bias):
    xq = mxq(f64(input), 2, "e4m3")
    wq = unpack_weight(weight_words, weight_scales, FMT)
    out = xq.reshape(B * S, K) @ wq
    return out.reshape(B, S, N) + f64(bias)

@@ -1,0 +1,142 @@
+from contextlib import ExitStack
+
+import concourse.mybir as mybir
+from concourse.masks import make_identity
+
+F32 = mybir.dt.float32
+BF16 = mybir.dt.bfloat16
+I32 = mybir.dt.int32
+U32 = mybir.dt.uint32
+U8 = mybir.dt.uint8
+FP8X4 = mybir.dt.float8_e4m3fn_x4
+
+P = 128
+PACK = 4
+K_GROUP = P * PACK
+
+TOKENS = 128
+K = 16384
+N = 1024
+GROUPS = K // K_GROUP
+N_BANK = 512
+BANKS = N // N_BANK
+
+WORD_PAIRS = 2
+X_LOAD_GROUPS = 8
+QUANT_GROUPS = 4
+BANK_GROUPS = 2
+
+SCALE_ROWS = 16
+SHARED = 4
+
+FLOPS = 2 * TOKENS * K * N
+
+
+def tile_tiledlinear_k_kernel(tc, x, weight_words, weight_scales, bias, out):
+    nc = tc.nc
+    x_rows = x.flatten_outer_dims()
+    out_rows = out.flatten_outer_dims()
+
+    with ExitStack() as ctx:
+        ctx.enter_context(tc.manual_schedule())
+        const = ctx.enter_context(tc.tile_pool(name="const", bufs=1))
+        x_pool = ctx.enter_context(tc.tile_pool(name="x", bufs=GROUPS // X_LOAD_GROUPS))
+        w_pool = ctx.enter_context(tc.tile_pool(name="w", bufs=GROUPS))
+        xq_pool = ctx.enter_context(tc.tile_pool(name="xq", bufs=GROUPS // QUANT_GROUPS))
+        stage = ctx.enter_context(tc.tile_pool(name="stage", bufs=3))
+        psum_acc = ctx.enter_context(tc.psum_pool(name="psum_acc", bufs=1))
+        psum_bias = ctx.enter_context(tc.psum_pool(name="psum_bias", bufs=BANKS))
+        psum_t = ctx.enter_context(tc.psum_pool(name="psum_t", bufs=4))
+
+        w_planes = const.tile([P, GROUPS // SHARED, N], U8, align_bytes=64)
+        nc.vector.memset(w_planes[:].bitcast(I32), 0)
+        bias_row = const.tile([P, N], BF16)
+        nc.vector.memset(bias_row[:], 0.0)
+        ones = const.tile([P, TOKENS], BF16)
+        nc.vector.memset(ones[:], 1.0)
+        ident = const.tile([P, P], F32)
+        make_identity(nc, ident[:])
+
+        x_loads = []
+        for c in range(GROUPS // X_LOAD_GROUPS):
+            x_load = x_pool.tile([P, X_LOAD_GROUPS * K_GROUP], BF16)
+            k_cols = slice(c * X_LOAD_GROUPS * K_GROUP, (c + 1) * X_LOAD_GROUPS * K_GROUP)
+            nc.sync.dma_start(out=x_load[:], in_=x_rows[:, k_cols])
+            x_loads.append(x_load)
+
+        nc.scalar.dma_start(out=bias_row[0:1, :], in_=bias.unsqueeze(0))
+
+        scale_rows = weight_scales.bitcast(F32).rearrange("(s j) q n -> q j s n", j=SHARED)
+        w_planes_f32 = w_planes[:].bitcast(F32)
+        for q in range(SCALE_ROWS):
+            top = 32 * (q // 4) + q % 4
+            nc.gpsimd.dma_start(out=w_planes_f32[top : top + 4 * SHARED : 4, :, :], in_=scale_rows[q])
+
+        w_tiles = []
+        for g in range(GROUPS):
+            w_words = w_pool.tile([P, N], U32, align_bytes=64)
+            nc.sync.dma_start(
+                out=w_words[:].bitcast(I32),
+                in_=weight_words[g].rearrange("p n t -> p (n t)").bitcast(I32),
+            )
+            w_tiles.append(w_words)
+
+        bias_all = const.tile([P, N], F32)
+        for h in range(BANKS):
+            n_cols = slice(h * N_BANK, (h + 1) * N_BANK)
+            bias_ps = psum_bias.tile([P, N_BANK], F32)
+            nc.tensor.matmul(out=bias_ps[:], lhsT=ones[:], rhs=bias_row[:, n_cols], start=True, stop=True)
+            nc.scalar.copy(out=bias_all[:, n_cols], in_=bias_ps[:])
+
+        x_codes = []
+        x_planes = []
+        for r in range(GROUPS // QUANT_GROUPS):
+            grouped = stage.tile([P, QUANT_GROUPS * TOKENS * PACK], BF16, align_bytes=64)
+            grouped_f32 = grouped[:].bitcast(F32)
+            for b in range(QUANT_GROUPS // BANK_GROUPS):
+                xt = psum_t.tile([P, BANK_GROUPS, WORD_PAIRS, TOKENS], F32)
+                for i in range(BANK_GROUPS):
+                    c, local = divmod(r * QUANT_GROUPS + b * BANK_GROUPS + i, X_LOAD_GROUPS)
+                    x_f32 = x_loads[c][:].bitcast(F32)
+                    first = local * P * WORD_PAIRS
+                    for u in range(WORD_PAIRS):
+                        nc.tensor.transpose(
+                            xt[:, i, u, :],
+                            x_f32[:, first + u : first + P * WORD_PAIRS : WORD_PAIRS],
+                            ident[:],
+                        )
+                bank_words = BANK_GROUPS * TOKENS * WORD_PAIRS
+                nc.scalar.copy(
+                    out=grouped_f32[:, b * bank_words : (b + 1) * bank_words].rearrange(
+                        "p (g m u) -> p g m u", g=BANK_GROUPS, u=WORD_PAIRS
+                    ),
+                    in_=xt[:].rearrange("p g u m -> p g m u"),
+                )
+            codes = xq_pool.tile([P, QUANT_GROUPS * TOKENS], U32, align_bytes=64)
+            plane = xq_pool.tile([P, QUANT_GROUPS * TOKENS], U8, align_bytes=64)
+            nc.vector.quantize_mx(out=codes[:].bitcast(FP8X4), scales=plane[:], in_=grouped[:])
+            x_codes.append(codes)
+            x_planes.append(plane)
+
+        acc = [psum_acc.tile([P, N_BANK], F32, name="acc%d" % h) for h in range(BANKS)]
+        for g in range(GROUPS):
+            r, slot = divmod(g, QUANT_GROUPS)
+            s, j = divmod(g, SHARED)
+            tokens = slice(slot * TOKENS, (slot + 1) * TOKENS)
+            for h in range(BANKS):
+                n_cols = slice(h * N_BANK, (h + 1) * N_BANK)
+                nc.tensor.matmul_mx(
+                    out=acc[h][:],
+                    lhsT=x_codes[r][:, tokens].bitcast(FP8X4),
+                    lhsT_scale=x_planes[r][:, tokens],
+                    rhs=w_tiles[g][:, n_cols].bitcast(FP8X4),
+                    rhs_scale=w_planes[4 * j : P, s, n_cols],
+                    start=(g == 0),
+                    stop=(g == GROUPS - 1),
+                )
+
+        for h in range(BANKS):
+            n_cols = slice(h * N_BANK, (h + 1) * N_BANK)
+            result = stage.tile([P, N_BANK], F32)
+            nc.vector.tensor_tensor(out=result[:], in0=acc[h][:], in1=bias_all[:, n_cols], op=mybir.AluOpType.add)
+            nc.sync.dma_start(out=out_rows[:, n_cols], in_=result[:])

@@ -26,7 +26,6 @@ X_LOAD_GROUPS = 8
 QUANT_GROUPS = 4
 BANK_GROUPS = 2
 
-SCALE_ROWS = 16
 SHARED = 4
 
 FLOPS = 2 * TOKENS * K * N
@@ -42,14 +41,18 @@ def tile_tiledlinear_k_kernel(tc, x, weight_words, weight_scales, bias, out):
         const = ctx.enter_context(tc.tile_pool(name="const", bufs=1))
         x_pool = ctx.enter_context(tc.tile_pool(name="x", bufs=GROUPS // X_LOAD_GROUPS))
         w_pool = ctx.enter_context(tc.tile_pool(name="w", bufs=GROUPS))
+        plane_pool = ctx.enter_context(tc.tile_pool(name="plane", bufs=GROUPS // SHARED))
         xq_pool = ctx.enter_context(tc.tile_pool(name="xq", bufs=GROUPS // QUANT_GROUPS))
         stage = ctx.enter_context(tc.tile_pool(name="stage", bufs=3))
         psum_acc = ctx.enter_context(tc.psum_pool(name="psum_acc", bufs=1))
         psum_bias = ctx.enter_context(tc.psum_pool(name="psum_bias", bufs=BANKS))
         psum_t = ctx.enter_context(tc.psum_pool(name="psum_t", bufs=4))
 
-        w_planes = const.tile([P, GROUPS // SHARED, N], U8, align_bytes=64)
-        nc.vector.memset(w_planes[:].bitcast(I32), 0)
+        w_planes = []
+        for s in range(GROUPS // SHARED):
+            w_plane = plane_pool.tile([P, N], U8, align_bytes=64)
+            nc.vector.memset(w_plane[:].bitcast(I32), 0)
+            w_planes.append(w_plane)
         bias_row = const.tile([P, N], BF16)
         nc.vector.memset(bias_row[:], 0.0)
         ones = const.tile([P, TOKENS], BF16)
@@ -66,11 +69,13 @@ def tile_tiledlinear_k_kernel(tc, x, weight_words, weight_scales, bias, out):
 
         nc.scalar.dma_start(out=bias_row[0:1, :], in_=bias.unsqueeze(0))
 
-        scale_rows = weight_scales.bitcast(F32).rearrange("(s j) q n -> q j s n", j=SHARED)
-        w_planes_f32 = w_planes[:].bitcast(F32)
-        for q in range(SCALE_ROWS):
-            top = 32 * (q // 4) + q % 4
-            nc.gpsimd.dma_start(out=w_planes_f32[top : top + 4 * SHARED : 4, :, :], in_=scale_rows[q])
+        scales_f32 = weight_scales.bitcast(F32)
+        for s in range(GROUPS // SHARED):
+            for quad in range(4):
+                nc.gpsimd.dma_start(
+                    out=w_planes[s][:].bitcast(F32)[32 * quad : 32 * quad + 4 * SHARED, :],
+                    in_=scales_f32[SHARED * s : SHARED * (s + 1), 4 * quad : 4 * quad + 4, :],
+                )
 
         w_tiles = []
         for g in range(GROUPS):
@@ -80,13 +85,6 @@ def tile_tiledlinear_k_kernel(tc, x, weight_words, weight_scales, bias, out):
                 in_=weight_words[g].rearrange("p n t -> p (n t)").bitcast(I32),
             )
             w_tiles.append(w_words)
-
-        bias_all = const.tile([P, N], F32)
-        for h in range(BANKS):
-            n_cols = slice(h * N_BANK, (h + 1) * N_BANK)
-            bias_ps = psum_bias.tile([P, N_BANK], F32)
-            nc.tensor.matmul(out=bias_ps[:], lhsT=ones[:], rhs=bias_row[:, n_cols], start=True, stop=True)
-            nc.scalar.copy(out=bias_all[:, n_cols], in_=bias_ps[:])
 
         x_codes = []
         x_planes = []
@@ -118,6 +116,13 @@ def tile_tiledlinear_k_kernel(tc, x, weight_words, weight_scales, bias, out):
             x_codes.append(codes)
             x_planes.append(plane)
 
+        bias_all = const.tile([P, N], F32)
+        for h in range(BANKS):
+            n_cols = slice(h * N_BANK, (h + 1) * N_BANK)
+            bias_ps = psum_bias.tile([P, N_BANK], F32)
+            nc.tensor.matmul(out=bias_ps[:], lhsT=ones[:], rhs=bias_row[:, n_cols], start=True, stop=True)
+            nc.scalar.copy(out=bias_all[:, n_cols], in_=bias_ps[:])
+
         acc = [psum_acc.tile([P, N_BANK], F32, name="acc%d" % h) for h in range(BANKS)]
         for g in range(GROUPS):
             r, slot = divmod(g, QUANT_GROUPS)
@@ -130,7 +135,7 @@ def tile_tiledlinear_k_kernel(tc, x, weight_words, weight_scales, bias, out):
                     lhsT=x_codes[r][:, tokens].bitcast(FP8X4),
                     lhsT_scale=x_planes[r][:, tokens],
                     rhs=w_tiles[g][:, n_cols].bitcast(FP8X4),
-                    rhs_scale=w_planes[4 * j : P, s, n_cols],
+                    rhs_scale=w_planes[s][4 * j : P, n_cols],
                     start=(g == 0),
                     stop=(g == GROUPS - 1),
                 )

@@ -26,6 +26,8 @@ X_LOAD_GROUPS = 8
 QUANT_GROUPS = 4
 BANK_GROUPS = 2
 
+W_LOADS = [4] * 7 + [1] * 4
+
 SHARED = 4
 
 FLOPS = 2 * TOKENS * K * N
@@ -40,7 +42,7 @@ def tile_tiledlinear_k_kernel(tc, x, weight_words, weight_scales, bias, out):
         ctx.enter_context(tc.manual_schedule())
         const = ctx.enter_context(tc.tile_pool(name="const", bufs=1))
         x_pool = ctx.enter_context(tc.tile_pool(name="x", bufs=GROUPS // X_LOAD_GROUPS))
-        w_pool = ctx.enter_context(tc.tile_pool(name="w", bufs=GROUPS))
+        w_pool = ctx.enter_context(tc.tile_pool(name="w", bufs=1))
         plane_pool = ctx.enter_context(tc.tile_pool(name="plane", bufs=GROUPS // SHARED))
         xq_pool = ctx.enter_context(tc.tile_pool(name="xq", bufs=GROUPS // QUANT_GROUPS))
         stage = ctx.enter_context(tc.tile_pool(name="stage", bufs=3))
@@ -78,13 +80,15 @@ def tile_tiledlinear_k_kernel(tc, x, weight_words, weight_scales, bias, out):
                 )
 
         w_tiles = []
-        for g in range(GROUPS):
-            w_words = w_pool.tile([P, N], U32, align_bytes=64)
+        g0 = 0
+        for c, count in enumerate(W_LOADS):
+            w_words = w_pool.tile([P, count, N], U32, align_bytes=64, name="w_load%d" % c)
             nc.sync.dma_start(
                 out=w_words[:].bitcast(I32),
-                in_=weight_words[g].rearrange("p n t -> p (n t)").bitcast(I32),
+                in_=weight_words[g0 : g0 + count].rearrange("g p n t -> p g (n t)").bitcast(I32),
             )
-            w_tiles.append(w_words)
+            w_tiles += [w_words[:, i, :] for i in range(count)]
+            g0 += count
 
         x_codes = []
         x_planes = []

@@ -20,13 +20,14 @@ N = 1024
 GROUPS = K // K_GROUP
 N_BANK = 512
 BANKS = N // N_BANK
+PIECES = [(0, 512), (512, 768), (768, 1024)]
 
 WORD_PAIRS = 2
 X_LOAD_GROUPS = 8
 QUANT_GROUPS = 4
 BANK_GROUPS = 2
 
-W_LOADS = [4] * 7 + [1] * 4
+W_LOADS = [4] * 7 + [1] * 3
 
 SHARED = 4
 
@@ -47,7 +48,7 @@ def tile_tiledlinear_k_kernel(tc, x, weight_words, weight_scales, bias, out):
         xq_pool = ctx.enter_context(tc.tile_pool(name="xq", bufs=GROUPS // QUANT_GROUPS))
         stage = ctx.enter_context(tc.tile_pool(name="stage", bufs=3))
         psum_acc = ctx.enter_context(tc.psum_pool(name="psum_acc", bufs=1))
-        psum_bias = ctx.enter_context(tc.psum_pool(name="psum_bias", bufs=BANKS))
+        psum_bias = ctx.enter_context(tc.psum_pool(name="psum_bias", bufs=1))
         psum_t = ctx.enter_context(tc.psum_pool(name="psum_t", bufs=4))
 
         w_planes = []
@@ -89,6 +90,14 @@ def tile_tiledlinear_k_kernel(tc, x, weight_words, weight_scales, bias, out):
             )
             w_tiles += [w_words[:, i, :] for i in range(count)]
             g0 += count
+        last_w = []
+        for lo, hi in PIECES:
+            w_words = w_pool.tile([P, hi - lo], U32, align_bytes=64, name="w_last%d" % lo)
+            nc.sync.dma_start(
+                out=w_words[:].bitcast(I32),
+                in_=weight_words[g0].rearrange("p n t -> p (n t)").bitcast(I32)[:, lo:hi],
+            )
+            last_w.append(w_words)
 
         x_codes = []
         x_planes = []
@@ -127,25 +136,24 @@ def tile_tiledlinear_k_kernel(tc, x, weight_words, weight_scales, bias, out):
             nc.tensor.matmul(out=bias_ps[:], lhsT=ones[:], rhs=bias_row[:, n_cols], start=True, stop=True)
             nc.scalar.copy(out=bias_all[:, n_cols], in_=bias_ps[:])
 
-        acc = [psum_acc.tile([P, N_BANK], F32, name="acc%d" % h) for h in range(BANKS)]
+        acc = [psum_acc.tile([P, hi - lo], F32, name="acc%d" % lo) for lo, hi in PIECES]
         for g in range(GROUPS):
             r, slot = divmod(g, QUANT_GROUPS)
             s, j = divmod(g, SHARED)
             tokens = slice(slot * TOKENS, (slot + 1) * TOKENS)
-            for h in range(BANKS):
-                n_cols = slice(h * N_BANK, (h + 1) * N_BANK)
+            for h, (lo, hi) in enumerate(PIECES):
+                words = w_tiles[g][:, lo:hi] if g < GROUPS - 1 else last_w[h][:]
                 nc.tensor.matmul_mx(
                     out=acc[h][:],
                     lhsT=x_codes[r][:, tokens].bitcast(FP8X4),
                     lhsT_scale=x_planes[r][:, tokens],
-                    rhs=w_tiles[g][:, n_cols].bitcast(FP8X4),
-                    rhs_scale=w_planes[s][4 * j : P, n_cols],
+                    rhs=words.bitcast(FP8X4),
+                    rhs_scale=w_planes[s][4 * j : P, lo:hi],
                     start=(g == 0),
                     stop=(g == GROUPS - 1),
                 )
 
-        for h in range(BANKS):
-            n_cols = slice(h * N_BANK, (h + 1) * N_BANK)
-            result = stage.tile([P, N_BANK], F32)
-            nc.vector.tensor_tensor(out=result[:], in0=acc[h][:], in1=bias_all[:, n_cols], op=mybir.AluOpType.add)
-            nc.sync.dma_start(out=out_rows[:, n_cols], in_=result[:])
+        for h, (lo, hi) in enumerate(PIECES):
+            result = stage.tile([P, hi - lo], F32, name="result")
+            nc.vector.tensor_tensor(out=result[:], in0=acc[h][:], in1=bias_all[:, lo:hi], op=mybir.AluOpType.add)
+            nc.sync.dma_start(out=out_rows[:, lo:hi], in_=result[:])

@@ -29,6 +29,7 @@ BANK_GROUPS = 2
 
 W_LOADS = [4] * 7 + [1] * 3
 
+SYNC_PLANES = 2
 SHARED = 4
 
 FLOPS = 2 * TOKENS * K * N
@@ -72,17 +73,21 @@ def tile_tiledlinear_k_kernel(tc, x, weight_words, weight_scales, bias, out):
 
         nc.scalar.dma_start(out=bias_row[0:1, :], in_=bias.unsqueeze(0))
 
-        scales_f32 = weight_scales.bitcast(F32)
-        for s in range(GROUPS // SHARED):
+        def load_scales(s, queue, dtype):
             for quad in range(4):
-                nc.gpsimd.dma_start(
-                    out=w_planes[s][:].bitcast(F32)[32 * quad : 32 * quad + 4 * SHARED, :],
-                    in_=scales_f32[SHARED * s : SHARED * (s + 1), 4 * quad : 4 * quad + 4, :],
+                queue.dma_start(
+                    out=w_planes[s][:].bitcast(dtype)[32 * quad : 32 * quad + 4 * SHARED, :],
+                    in_=weight_scales.bitcast(dtype)[SHARED * s : SHARED * (s + 1), 4 * quad : 4 * quad + 4, :],
                 )
+
+        for s in range(SYNC_PLANES, GROUPS // SHARED):
+            load_scales(s, nc.gpsimd, F32)
 
         w_tiles = []
         g0 = 0
         for c, count in enumerate(W_LOADS):
+            if g0 % SHARED == 0 and g0 // SHARED < SYNC_PLANES:
+                load_scales(g0 // SHARED, nc.sync, I32)
             w_words = w_pool.tile([P, count, N], U32, align_bytes=64, name="w_load%d" % c)
             nc.sync.dma_start(
                 out=w_words[:].bitcast(I32),

@@ -27,7 +27,7 @@ X_LOAD_GROUPS = 8
 QUANT_GROUPS = 4
 BANK_GROUPS = 2
 
-W_LOADS = [4] * 7 + [1] * 3
+W_LOADS = [2] * 14 + [1] * 3
 
 SYNC_PLANES = 2
 SHARED = 4

from contextlib import ExitStack

import concourse.mybir as mybir
from concourse.masks import make_identity

F32 = mybir.dt.float32
BF16 = mybir.dt.bfloat16
I32 = mybir.dt.int32
U32 = mybir.dt.uint32
U8 = mybir.dt.uint8
FP8X4 = mybir.dt.float8_e4m3fn_x4

P = 128
PACK = 4
K_GROUP = P * PACK

TOKENS = 128
K = 16384
N = 1024
GROUPS = K // K_GROUP
N_BANK = 512
BANKS = N // N_BANK
PIECES = [(0, 512), (512, 768), (768, 1024)]

WORD_PAIRS = 2
X_LOAD_GROUPS = 8
QUANT_GROUPS = 4
BANK_GROUPS = 2

W_LOADS = [2] * 14 + [1] * 3

SYNC_PLANES = 2
SHARED = 4

FLOPS = 2 * TOKENS * K * N


def tile_tiledlinear_k_kernel(tc, x, weight_words, weight_scales, bias, out):
    nc = tc.nc
    x_rows = x.flatten_outer_dims()
    out_rows = out.flatten_outer_dims()

    with ExitStack() as ctx:
        ctx.enter_context(tc.manual_schedule())
        const = ctx.enter_context(tc.tile_pool(name="const", bufs=1))
        x_pool = ctx.enter_context(tc.tile_pool(name="x", bufs=GROUPS // X_LOAD_GROUPS))
        w_pool = ctx.enter_context(tc.tile_pool(name="w", bufs=1))
        plane_pool = ctx.enter_context(tc.tile_pool(name="plane", bufs=GROUPS // SHARED))
        xq_pool = ctx.enter_context(tc.tile_pool(name="xq", bufs=GROUPS // QUANT_GROUPS))
        stage = ctx.enter_context(tc.tile_pool(name="stage", bufs=3))
        psum_acc = ctx.enter_context(tc.psum_pool(name="psum_acc", bufs=1))
        psum_bias = ctx.enter_context(tc.psum_pool(name="psum_bias", bufs=1))
        psum_t = ctx.enter_context(tc.psum_pool(name="psum_t", bufs=4))

        w_planes = []
        for s in range(GROUPS // SHARED):
            w_plane = plane_pool.tile([P, N], U8, align_bytes=64)
            nc.vector.memset(w_plane[:].bitcast(I32), 0)
            w_planes.append(w_plane)
        bias_row = const.tile([P, N], BF16)
        nc.vector.memset(bias_row[:], 0.0)
        ones = const.tile([P, TOKENS], BF16)
        nc.vector.memset(ones[:], 1.0)
        ident = const.tile([P, P], F32)
        make_identity(nc, ident[:])

        x_loads = []
        for c in range(GROUPS // X_LOAD_GROUPS):
            x_load = x_pool.tile([P, X_LOAD_GROUPS * K_GROUP], BF16)
            k_cols = slice(c * X_LOAD_GROUPS * K_GROUP, (c + 1) * X_LOAD_GROUPS * K_GROUP)
            nc.sync.dma_start(out=x_load[:], in_=x_rows[:, k_cols])
            x_loads.append(x_load)

        nc.scalar.dma_start(out=bias_row[0:1, :], in_=bias.unsqueeze(0))

        def load_scales(s, queue, dtype):
            for quad in range(4):
                queue.dma_start(
                    out=w_planes[s][:].bitcast(dtype)[32 * quad : 32 * quad + 4 * SHARED, :],
                    in_=weight_scales.bitcast(dtype)[SHARED * s : SHARED * (s + 1), 4 * quad : 4 * quad + 4, :],
                )

        for s in range(SYNC_PLANES, GROUPS // SHARED):
            load_scales(s, nc.gpsimd, F32)

        w_tiles = []
        g0 = 0
        for c, count in enumerate(W_LOADS):
            if g0 % SHARED == 0 and g0 // SHARED < SYNC_PLANES:
                load_scales(g0 // SHARED, nc.sync, I32)
            w_words = w_pool.tile([P, count, N], U32, align_bytes=64, name="w_load%d" % c)
            nc.sync.dma_start(
                out=w_words[:].bitcast(I32),
                in_=weight_words[g0 : g0 + count].rearrange("g p n t -> p g (n t)").bitcast(I32),
            )
            w_tiles += [w_words[:, i, :] for i in range(count)]
            g0 += count
        last_w = []
        for lo, hi in PIECES:
            w_words = w_pool.tile([P, hi - lo], U32, align_bytes=64, name="w_last%d" % lo)
            nc.sync.dma_start(
                out=w_words[:].bitcast(I32),
                in_=weight_words[g0].rearrange("p n t -> p (n t)").bitcast(I32)[:, lo:hi],
            )
            last_w.append(w_words)

        x_codes = []
        x_planes = []
        for r in range(GROUPS // QUANT_GROUPS):
            grouped = stage.tile([P, QUANT_GROUPS * TOKENS * PACK], BF16, align_bytes=64)
            grouped_f32 = grouped[:].bitcast(F32)
            for b in range(QUANT_GROUPS // BANK_GROUPS):
                xt = psum_t.tile([P, BANK_GROUPS, WORD_PAIRS, TOKENS], F32)
                for i in range(BANK_GROUPS):
                    c, local = divmod(r * QUANT_GROUPS + b * BANK_GROUPS + i, X_LOAD_GROUPS)
                    x_f32 = x_loads[c][:].bitcast(F32)
                    first = local * P * WORD_PAIRS
                    for u in range(WORD_PAIRS):
                        nc.tensor.transpose(
                            xt[:, i, u, :],
                            x_f32[:, first + u : first + P * WORD_PAIRS : WORD_PAIRS],
                            ident[:],
                        )
                bank_words = BANK_GROUPS * TOKENS * WORD_PAIRS
                nc.scalar.copy(
                    out=grouped_f32[:, b * bank_words : (b + 1) * bank_words].rearrange(
                        "p (g m u) -> p g m u", g=BANK_GROUPS, u=WORD_PAIRS
                    ),
                    in_=xt[:].rearrange("p g u m -> p g m u"),
                )
            codes = xq_pool.tile([P, QUANT_GROUPS * TOKENS], U32, align_bytes=64)
            plane = xq_pool.tile([P, QUANT_GROUPS * TOKENS], U8, align_bytes=64)
            nc.vector.quantize_mx(out=codes[:].bitcast(FP8X4), scales=plane[:], in_=grouped[:])
            x_codes.append(codes)
            x_planes.append(plane)

        bias_all = const.tile([P, N], F32)
        for h in range(BANKS):
            n_cols = slice(h * N_BANK, (h + 1) * N_BANK)
            bias_ps = psum_bias.tile([P, N_BANK], F32)
            nc.tensor.matmul(out=bias_ps[:], lhsT=ones[:], rhs=bias_row[:, n_cols], start=True, stop=True)
            nc.scalar.copy(out=bias_all[:, n_cols], in_=bias_ps[:])

        acc = [psum_acc.tile([P, hi - lo], F32, name="acc%d" % lo) for lo, hi in PIECES]
        for g in range(GROUPS):
            r, slot = divmod(g, QUANT_GROUPS)
            s, j = divmod(g, SHARED)
            tokens = slice(slot * TOKENS, (slot + 1) * TOKENS)
            for h, (lo, hi) in enumerate(PIECES):
                words = w_tiles[g][:, lo:hi] if g < GROUPS - 1 else last_w[h][:]
                nc.tensor.matmul_mx(
                    out=acc[h][:],
                    lhsT=x_codes[r][:, tokens].bitcast(FP8X4),
                    lhsT_scale=x_planes[r][:, tokens],
                    rhs=words.bitcast(FP8X4),
                    rhs_scale=w_planes[s][4 * j : P, lo:hi],
                    start=(g == 0),
                    stop=(g == GROUPS - 1),
                )

        for h, (lo, hi) in enumerate(PIECES):
            result = stage.tile([P, hi - lo], F32, name="result")
            nc.vector.tensor_tensor(out=result[:], in0=acc[h][:], in1=bias_all[:, lo:hi], op=mybir.AluOpType.add)
            nc.sync.dma_start(out=out_rows[:, lo:hi], in_=result[:])
